import numpy as np
import ml_dtypes


def mxq(x, axis, fmt="e4m3"):
    dtype, down = {"e4m3": (ml_dtypes.float8_e4m3fn, 7), "e5m2": (ml_dtypes.float8_e5m2, 14)}[fmt]
    v = np.moveaxis(np.asarray(x, np.float32).astype(ml_dtypes.bfloat16).astype(np.float64), axis, -1)
    blocks = v.reshape(v.shape[:-1] + (-1, 32))
    amax = np.abs(blocks).max(-1, keepdims=True)
    byte = np.maximum(np.where(amax > 0, np.frexp(amax)[1] - 1 + 127, 0) - down, 1)
    scale = np.exp2(byte - 127.0)
    codes = (blocks / scale).astype(np.float32).astype(dtype).astype(np.float64)
    return np.moveaxis((codes * scale).reshape(v.shape), -1, axis)


WIDE = False


def mx_kscale(k):
    if not WIDE:
        return np.ones(k)
    levels = np.array([10, -10, 5, -5, 0])
    a = np.random.permutation(np.resize(levels, k // 512 * 4)).reshape(k // 512, 4)
    idx = np.arange(k)
    return np.exp2(a[idx // 512, idx % 128 // 32])


BF16 = ml_dtypes.bfloat16


def bf(x):
    return np.asarray(x, np.float32).astype(BF16)


def f64(x):
    return np.asarray(x).astype(np.float64)


E2M1 = np.array([0.0, 0.5, 1.0, 1.5, 2.0, 3.0, 4.0, 6.0, -0.0, -0.5, -1.0, -1.5, -2.0, -3.0, -4.0, -6.0])


def pack_weight(w, fmt):
    k, n = w.shape
    w = f64(bf(w)).reshape(k // 32, 32, n)
    amax = np.abs(w).max(1)
    if fmt == "e4m3":
        byte = np.frexp(amax)[1] - 1 + 127 - 7
    else:
        mant, ex = np.frexp(amax / 6.0)
        byte = np.where(mant > 0.5, ex, ex - 1) + 127
    byte = np.clip(np.where(amax > 0, byte, 1), 1, 254)
    scaled = (w * np.exp2(127.0 - byte)[:, None, :]).reshape(k, n).astype(np.float32)
    by_word = np.ascontiguousarray(scaled.reshape(k // 512, 128, 4, n).transpose(0, 1, 3, 2))
    if fmt == "e4m3":
        words = by_word.astype(ml_dtypes.float8_e4m3fn).view(np.uint8)
    else:
        c = by_word.astype(ml_dtypes.float4_e2m1fn).view(np.uint8) & 0xF
        words = c[..., 0::2] | (c[..., 1::2] << 4)
    return np.ascontiguousarray(words), np.ascontiguousarray(byte.astype(np.uint8).reshape(k // 512, 16, n))


def unpack_weight(words, scales, fmt):
    g, p, n, _ = words.shape
    if fmt == "e4m3":
        vals = np.ascontiguousarray(words).view(ml_dtypes.float8_e4m3fn).astype(np.float64)
    else:
        nib = np.empty((g, p, n, 4), np.uint8)
        nib[..., 0::2] = words & 0xF
        nib[..., 1::2] = words >> 4
        vals = E2M1[nib]
    vals = vals * np.repeat(np.exp2(scales.astype(np.float64) - 127.0), 8, axis=1)[..., None]
    return vals.transpose(0, 1, 3, 2).reshape(g * 512, n)

def pack4(w):
    words, scales = pack_weight(w, "e2m1")
    return words.reshape(words.shape[0], 128, -1), scales


def unpack4(words, scales):
    return unpack_weight(words.reshape(words.shape[0], 128, -1, 2), scales, "e2m1")


B, C, S, OUT = 256, 4, 64, 128
IN = C * S * S
HS = S // 2
SUB, BLK = 4, 32


def haar_dwt2_features(x):
    x4 = x.reshape(x.shape[0], C, S, S)
    a = x4[:, :, 0::2, 0::2]
    bq = x4[:, :, 0::2, 1::2]
    c = x4[:, :, 1::2, 0::2]
    d = x4[:, :, 1::2, 1::2]
    LL = (a + bq + c + d) * 0.5
    LH = (a + bq - c - d) * 0.5
    HL = (a - bq + c - d) * 0.5
    HH = (a - bq - c + d) * 0.5
    t = np.stack([LL, LH, HL, HH], axis=2)
    return t.reshape(x.shape[0], -1)


def setup_inputs():
    g = mx_kscale(IN).reshape(-1, SUB, BLK)[:, 0, :].reshape(C, HS, HS)
    gx = np.repeat(np.repeat(g, 2, axis=1), 2, axis=2).reshape(IN)
    gt = np.repeat(g[:, None], SUB, axis=1).reshape(IN)
    x = bf(np.random.standard_normal((B, IN)) * gx)
    w = np.random.standard_normal((OUT, IN)) * (1.0 / np.sqrt(IN)) / gt
    words, scales = pack4(np.ascontiguousarray(w.T))
    b = bf(np.random.standard_normal(OUT) * 0.5)
    return {"x": x, "W_words": words, "W_scales": scales, "b": b}


def reference(x, W_words, W_scales, b):
    t = haar_dwt2_features(f64(x))
    return (mxq(t, 1, "e4m3") @ unpack4(W_words, W_scales)) + f64(b)

@@ -1,0 +1,167 @@
+from contextlib import ExitStack
+
+import concourse.mybir as mybir
+from concourse.masks import make_identity
+
+F32 = mybir.dt.float32
+BF16 = mybir.dt.bfloat16
+I32 = mybir.dt.int32
+U32 = mybir.dt.uint32
+U8 = mybir.dt.uint8
+FP8X4 = mybir.dt.float8_e4m3fn_x4
+FP4X4 = mybir.dt.float4_e2m1fn_x4
+ADD = mybir.AluOpType.add
+SUBTRACT = mybir.AluOpType.subtract
+COPY = mybir.ActivationFunctionType.Copy
+
+P = 128
+PACK = 4
+K_PASS = P * PACK
+
+BATCH, CHANNELS, SIDE, OUT = 256, 4, 64, 128
+HALF_SIDE = SIDE // 2
+PIXELS = SIDE * SIDE
+BAND = HALF_SIDE * HALF_SIDE
+SUBBANDS = 4
+PASSES = CHANNELS * SUBBANDS * BAND // K_PASS
+BAND_PASSES = BAND // K_PASS
+ROW_TILES = BATCH // P
+WORDS_PER_ROW = HALF_SIDE // PACK
+
+SIGNS = 2
+STAGES = ROW_TILES * CHANNELS * SIGNS
+STAGE_PASSES = 2 * BAND_PASSES
+QUANTISE_LAG = 2
+FINISH_LAG = 3
+
+FLOPS = 2 * BATCH * CHANNELS * PIXELS * OUT
+
+
+def tile_waveletlinearlayer_kernel(tc, x, W_words, W_scales, b, out):
+    nc = tc.nc
+    with ExitStack() as ctx:
+        const = ctx.enter_context(tc.tile_pool(name="const", bufs=1))
+        step1 = ctx.enter_context(tc.tile_pool(name="step1", bufs=3))
+        packed = ctx.enter_context(tc.tile_pool(name="packed", bufs=3))
+        results = ctx.enter_context(tc.tile_pool(name="results", bufs=2))
+        banks = ctx.enter_context(tc.psum_pool(name="banks", bufs=6))
+        sums = ctx.enter_context(tc.psum_pool(name="sums", bufs=2))
+        ctx.enter_context(tc.manual_schedule())
+
+        identity = const.tile([P, P], F32)
+        make_identity(nc, identity[:])
+
+        pixel_tiles = {}
+
+        def load_pixels(row_tile, channel):
+            pixels = const.tile([P, PIXELS], BF16, name="pixels_%d_%d" % (row_tile, channel))
+            nc.sync.dma_start(
+                out=pixels[:],
+                in_=x[row_tile * P : (row_tile + 1) * P, channel * PIXELS : (channel + 1) * PIXELS],
+            )
+            pixel_tiles[(row_tile, channel)] = pixels
+
+        w_scales = const.tile([P, PASSES, OUT], U8, align_bytes=64)
+        nc.vector.memset(w_scales[:].bitcast(I32), 0)
+        w_codes = const.tile([P, PASSES, 2 * OUT], U8, align_bytes=64)
+        bias = const.tile([P, OUT], BF16)
+
+        load_pixels(0, 0)
+        load_pixels(0, 1)
+        for quadrant in range(4):
+            nc.sync.dma_start(
+                out=w_scales[32 * quadrant : 32 * quadrant + 4].bitcast(I32),
+                in_=W_scales[:, 4 * quadrant : 4 * quadrant + 4, :].bitcast(I32).rearrange("g r w -> r g w"),
+            )
+        nc.sync.dma_start(out=w_codes[:].bitcast(I32), in_=W_words.bitcast(I32).rearrange("g p w -> p g w"))
+        nc.sync.dma_start(out=bias[:], in_=b.partition_broadcast(P))
+        for row_tile in range(ROW_TILES):
+            for channel in range(CHANNELS):
+                if (row_tile, channel) not in pixel_tiles:
+                    load_pixels(row_tile, channel)
+
+        def place(stage):
+            row_tile, rest = divmod(stage, CHANNELS * SIGNS)
+            channel, sign = divmod(rest, SIGNS)
+            return row_tile, channel, sign
+
+        def pair_columns(stage, image_row, target):
+            row_tile, channel, sign = place(stage)
+            pairs = pixel_tiles[(row_tile, channel)][:].rearrange(
+                "n (i r c t e) -> n r e i c t", i=HALF_SIDE, r=2, c=WORDS_PER_ROW, t=PACK, e=2
+            )
+            nc.vector.tensor_tensor(
+                out=target[:].rearrange("n t (i c) -> n i c t", c=WORDS_PER_ROW),
+                in0=pairs[:, image_row, 0],
+                in1=pairs[:, image_row, 1],
+                op=(ADD if sign == 0 else SUBTRACT),
+            )
+
+        def transpose_and_add(first, second, half, grouped_slot):
+            bank = banks.tile([P, PACK, P], F32)
+            features = slice(half * P, (half + 1) * P)
+            for t in range(PACK):
+                nc.tensor.matmul(
+                    out=bank[:, t, :], lhsT=first[:, t, features], rhs=identity[:],
+                    is_transpose=True, start=True, stop=False,
+                )
+                nc.tensor.matmul(
+                    out=bank[:, t, :], lhsT=second[:, t, features], rhs=identity[:],
+                    is_transpose=True, start=False, stop=True,
+                )
+            nc.scalar.activation(out=grouped_slot, in_=bank[:].rearrange("p t n -> p n t"), func=COPY, scale=0.5)
+
+        grouped_tiles = {}
+        sum_tiles = {}
+
+        def quantise_and_multiply(stage):
+            row_tile, channel, sign = place(stage)
+            grouped = grouped_tiles.pop(stage)
+            t_codes = packed.tile([P, STAGE_PASSES, P], U32, align_bytes=64)
+            t_scales = packed.tile([P, STAGE_PASSES, P], U8, align_bytes=64)
+            nc.vector.quantize_mx(
+                out=t_codes[:].rearrange("p s n -> p (s n)").bitcast(FP8X4),
+                scales=t_scales[:].rearrange("p s n -> p (s n)"),
+                in_=grouped[:].rearrange("p s n t -> p (s n t)"),
+            )
+            if stage % (CHANNELS * SIGNS) == 0:
+                sum_tiles[row_tile] = sums.tile([P, OUT], F32, name="batch_sum")
+            for slot in range(STAGE_PASSES):
+                difference, half = divmod(slot, BAND_PASSES)
+                subband = 2 * sign + difference
+                g = (channel * SUBBANDS + subband) * BAND_PASSES + half
+                nc.tensor.matmul_mx(
+                    out=sum_tiles[row_tile][:],
+                    lhsT=t_codes[:, slot, :].bitcast(FP8X4),
+                    lhsT_scale=t_scales[:, slot, :],
+                    rhs=w_codes[:, g, :].bitcast(FP4X4),
+                    rhs_scale=w_scales[:, g, :],
+                    start=(stage % (CHANNELS * SIGNS) == 0 and slot == 0),
+                    stop=(stage % (CHANNELS * SIGNS) == CHANNELS * SIGNS - 1 and slot == STAGE_PASSES - 1),
+                )
+
+        def finish(row_tile):
+            result = results.tile([P, OUT], F32)
+            nc.vector.tensor_tensor(out=result[:], in0=sum_tiles[row_tile][:], in1=bias[:], op=ADD)
+            nc.sync.dma_start(out=out[row_tile * P : (row_tile + 1) * P, :], in_=result[:])
+
+        for step in range(STAGES + FINISH_LAG):
+            if step < STAGES:
+                even = step1.tile([P, PACK, BAND // PACK], F32)
+                odd = step1.tile([P, PACK, BAND // PACK], F32)
+                minus_odd = step1.tile([P, PACK, BAND // PACK], F32)
+                pair_columns(step, 0, even)
+            finished = step - FINISH_LAG
+            if finished >= 0 and (finished + 1) % (CHANNELS * SIGNS) == 0:
+                finish(finished // (CHANNELS * SIGNS))
+            if step < STAGES:
+                pair_columns(step, 1, odd)
+                nc.scalar.activation(out=minus_odd[:], in_=odd[:], func=COPY, scale=-1.0)
+            if 0 <= step - QUANTISE_LAG < STAGES:
+                quantise_and_multiply(step - QUANTISE_LAG)
+            if step < STAGES:
+                grouped = packed.tile([P, STAGE_PASSES, P, PACK], BF16, align_bytes=64)
+                grouped_tiles[step] = grouped
+                for slot in range(STAGE_PASSES):
+                    difference, half = divmod(slot, BAND_PASSES)
+                    transpose_and_add(even, minus_odd if difference else odd, half, grouped[:, slot])

@@ -25,14 +25,20 @@ BAND = HALF_SIDE * HALF_SIDE
 SUBBANDS = 4
 PASSES = CHANNELS * SUBBANDS * BAND // K_PASS
 BAND_PASSES = BAND // K_PASS
+PASS_ROWS = HALF_SIDE // BAND_PASSES
+PASS_PIXELS = PIXELS // BAND_PASSES
 ROW_TILES = BATCH // P
 WORDS_PER_ROW = HALF_SIDE // PACK
 
 SIGNS = 2
-STAGES = ROW_TILES * CHANNELS * SIGNS
-STAGE_PASSES = 2 * BAND_PASSES
+TILE_STAGES = CHANNELS * BAND_PASSES * SIGNS
+STAGES = ROW_TILES * TILE_STAGES
+STAGE_PASSES = 2
 QUANTISE_LAG = 2
+RUN_STAGES = 4
 FINISH_LAG = 3
+
+EARLY_PIECES = 3
 
 FLOPS = 2 * BATCH * CHANNELS * PIXELS * OUT
 
@@ -41,8 +47,8 @@ def tile_waveletlinearlayer_kernel(tc, x, W_words, W_scales, b, out):
     nc = tc.nc
     with ExitStack() as ctx:
         const = ctx.enter_context(tc.tile_pool(name="const", bufs=1))
-        step1 = ctx.enter_context(tc.tile_pool(name="step1", bufs=3))
-        packed = ctx.enter_context(tc.tile_pool(name="packed", bufs=3))
+        step1 = ctx.enter_context(tc.tile_pool(name="step1", bufs=4))
+        packed = ctx.enter_context(tc.tile_pool(name="packed", bufs=6))
         results = ctx.enter_context(tc.tile_pool(name="results", bufs=2))
         banks = ctx.enter_context(tc.psum_pool(name="banks", bufs=6))
         sums = ctx.enter_context(tc.psum_pool(name="sums", bufs=2))
@@ -53,21 +59,22 @@ def tile_waveletlinearlayer_kernel(tc, x, W_words, W_scales, b, out):
 
         pixel_tiles = {}
 
-        def load_pixels(row_tile, channel):
-            pixels = const.tile([P, PIXELS], BF16, name="pixels_%d_%d" % (row_tile, channel))
+        def load_pixels(piece):
+            row_tile, columns = divmod(piece, CHANNELS * BAND_PASSES)
+            pixels = const.tile([P, PASS_PIXELS], BF16, name="pixels_%d" % piece)
             nc.sync.dma_start(
                 out=pixels[:],
-                in_=x[row_tile * P : (row_tile + 1) * P, channel * PIXELS : (channel + 1) * PIXELS],
+                in_=x[row_tile * P : (row_tile + 1) * P, columns * PASS_PIXELS : (columns + 1) * PASS_PIXELS],
             )
-            pixel_tiles[(row_tile, channel)] = pixels
+            pixel_tiles[piece] = pixels
 
         w_scales = const.tile([P, PASSES, OUT], U8, align_bytes=64)
         nc.vector.memset(w_scales[:].bitcast(I32), 0)
         w_codes = const.tile([P, PASSES, 2 * OUT], U8, align_bytes=64)
         bias = const.tile([P, OUT], BF16)
 
-        load_pixels(0, 0)
-        load_pixels(0, 1)
+        for piece in range(EARLY_PIECES):
+            load_pixels(piece)
         for quadrant in range(4):
             nc.sync.dma_start(
                 out=w_scales[32 * quadrant : 32 * quadrant + 4].bitcast(I32),
@@ -75,20 +82,14 @@ def tile_waveletlinearlayer_kernel(tc, x, W_words, W_scales, b, out):
             )
         nc.sync.dma_start(out=w_codes[:].bitcast(I32), in_=W_words.bitcast(I32).rearrange("g p w -> p g w"))
         nc.sync.dma_start(out=bias[:], in_=b.partition_broadcast(P))
-        for row_tile in range(ROW_TILES):
-            for channel in range(CHANNELS):
-                if (row_tile, channel) not in pixel_tiles:
-                    load_pixels(row_tile, channel)
+        for piece in range(EARLY_PIECES, STAGES // SIGNS):
+            load_pixels(piece)
 
-        def place(stage):
-            row_tile, rest = divmod(stage, CHANNELS * SIGNS)
-            channel, sign = divmod(rest, SIGNS)
-            return row_tile, channel, sign
 
         def pair_columns(stage, image_row, target):
-            row_tile, channel, sign = place(stage)
-            pairs = pixel_tiles[(row_tile, channel)][:].rearrange(
-                "n (i r c t e) -> n r e i c t", i=HALF_SIDE, r=2, c=WORDS_PER_ROW, t=PACK, e=2
+            piece, sign = divmod(stage, SIGNS)
+            pairs = pixel_tiles[piece][:].rearrange(
+                "n (i r c t e) -> n r e i c t", i=PASS_ROWS, r=2, c=WORDS_PER_ROW, t=PACK, e=2
             )
             nc.vector.tensor_tensor(
                 out=target[:].rearrange("n t (i c) -> n i c t", c=WORDS_PER_ROW),
@@ -97,16 +98,15 @@ def tile_waveletlinearlayer_kernel(tc, x, W_words, W_scales, b, out):
                 op=(ADD if sign == 0 else SUBTRACT),
             )
 
-        def transpose_and_add(first, second, half, grouped_slot):
+        def transpose_and_add(first, second, grouped_slot):
             bank = banks.tile([P, PACK, P], F32)
-            features = slice(half * P, (half + 1) * P)
             for t in range(PACK):
                 nc.tensor.matmul(
-                    out=bank[:, t, :], lhsT=first[:, t, features], rhs=identity[:],
+                    out=bank[:, t, :], lhsT=first[:, t, :], rhs=identity[:],
                     is_transpose=True, start=True, stop=False,
                 )
                 nc.tensor.matmul(
-                    out=bank[:, t, :], lhsT=second[:, t, features], rhs=identity[:],
+                    out=bank[:, t, :], lhsT=second[:, t, :], rhs=identity[:],
                     is_transpose=True, start=False, stop=True,
                 )
             nc.scalar.activation(out=grouped_slot, in_=bank[:].rearrange("p t n -> p n t"), func=COPY, scale=0.5)
@@ -114,8 +114,9 @@ def tile_waveletlinearlayer_kernel(tc, x, W_words, W_scales, b, out):
         grouped_tiles = {}
         sum_tiles = {}
 
-        def quantise_and_multiply(stage):
-            row_tile, channel, sign = place(stage)
+        code_tiles = {}
+
+        def quantise(stage):
             grouped = grouped_tiles.pop(stage)
             t_codes = packed.tile([P, STAGE_PASSES, P], U32, align_bytes=64)
             t_scales = packed.tile([P, STAGE_PASSES, P], U8, align_bytes=64)
@@ -124,20 +125,26 @@ def tile_waveletlinearlayer_kernel(tc, x, W_words, W_scales, b, out):
                 scales=t_scales[:].rearrange("p s n -> p (s n)"),
                 in_=grouped[:].rearrange("p s n t -> p (s n t)"),
             )
-            if stage % (CHANNELS * SIGNS) == 0:
+            code_tiles[stage] = (t_codes, t_scales)
+
+        def multiply(stage):
+            row_tile, tile_stage = divmod(stage, TILE_STAGES)
+            channel, rest = divmod(tile_stage, BAND_PASSES * SIGNS)
+            half, sign = divmod(rest, SIGNS)
+            t_codes, t_scales = code_tiles.pop(stage)
+            if tile_stage == 0:
                 sum_tiles[row_tile] = sums.tile([P, OUT], F32, name="batch_sum")
-            for slot in range(STAGE_PASSES):
-                difference, half = divmod(slot, BAND_PASSES)
+            for difference in range(STAGE_PASSES):
                 subband = 2 * sign + difference
                 g = (channel * SUBBANDS + subband) * BAND_PASSES + half
                 nc.tensor.matmul_mx(
                     out=sum_tiles[row_tile][:],
-                    lhsT=t_codes[:, slot, :].bitcast(FP8X4),
-                    lhsT_scale=t_scales[:, slot, :],
+                    lhsT=t_codes[:, difference, :].bitcast(FP8X4),
+                    lhsT_scale=t_scales[:, difference, :],
                     rhs=w_codes[:, g, :].bitcast(FP4X4),
                     rhs_scale=w_scales[:, g, :],
-                    start=(stage % (CHANNELS * SIGNS) == 0 and slot == 0),
-                    stop=(stage % (CHANNELS * SIGNS) == CHANNELS * SIGNS - 1 and slot == STAGE_PASSES - 1),
+                    start=(tile_stage == 0 and difference == 0),
+                    stop=(tile_stage == TILE_STAGES - 1 and difference == STAGE_PASSES - 1),
                 )
 
         def finish(row_tile):
@@ -145,23 +152,29 @@ def tile_waveletlinearlayer_kernel(tc, x, W_words, W_scales, b, out):
             nc.vector.tensor_tensor(out=result[:], in0=sum_tiles[row_tile][:], in1=bias[:], op=ADD)
             nc.sync.dma_start(out=out[row_tile * P : (row_tile + 1) * P, :], in_=result[:])
 
+        waiting = []
         for step in range(STAGES + FINISH_LAG):
             if step < STAGES:
-                even = step1.tile([P, PACK, BAND // PACK], F32)
-                odd = step1.tile([P, PACK, BAND // PACK], F32)
-                minus_odd = step1.tile([P, PACK, BAND // PACK], F32)
+                even = step1.tile([P, PACK, P], F32)
+                odd = step1.tile([P, PACK, P], F32)
+                minus_odd = step1.tile([P, PACK, P], F32)
                 pair_columns(step, 0, even)
             finished = step - FINISH_LAG
-            if finished >= 0 and (finished + 1) % (CHANNELS * SIGNS) == 0:
-                finish(finished // (CHANNELS * SIGNS))
+            if finished >= 0 and (finished + 1) % TILE_STAGES == 0:
+                finish(finished // TILE_STAGES)
             if step < STAGES:
                 pair_columns(step, 1, odd)
                 nc.scalar.activation(out=minus_odd[:], in_=odd[:], func=COPY, scale=-1.0)
-            if 0 <= step - QUANTISE_LAG < STAGES:
-                quantise_and_multiply(step - QUANTISE_LAG)
+            quantised = step - QUANTISE_LAG
+            if 0 <= quantised < STAGES:
+                quantise(quantised)
+                waiting.append(quantised)
+                if len(waiting) == RUN_STAGES or step >= STAGES:
+                    for stage in waiting:
+                        multiply(stage)
+                    waiting = []
             if step < STAGES:
                 grouped = packed.tile([P, STAGE_PASSES, P, PACK], BF16, align_bytes=64)
                 grouped_tiles[step] = grouped
-                for slot in range(STAGE_PASSES):
-                    difference, half = divmod(slot, BAND_PASSES)
-                    transpose_and_add(even, minus_odd if difference else odd, half, grouped[:, slot])
+                transpose_and_add(even, odd, grouped[:, 0])
+                transpose_and_add(even, minus_odd, grouped[:, 1])

@@ -12,6 +12,7 @@ FP8X4 = mybir.dt.float8_e4m3fn_x4
 FP4X4 = mybir.dt.float4_e2m1fn_x4
 ADD = mybir.AluOpType.add
 SUBTRACT = mybir.AluOpType.subtract
+MULT = mybir.AluOpType.mult
 COPY = mybir.ActivationFunctionType.Copy
 
 P = 128
@@ -34,11 +35,15 @@ SIGNS = 2
 TILE_STAGES = CHANNELS * BAND_PASSES * SIGNS
 STAGES = ROW_TILES * TILE_STAGES
 STAGE_PASSES = 2
-QUANTISE_LAG = 2
+VECTOR_EVERY = 3
 RUN_STAGES = 4
-FINISH_LAG = 3
-
 EARLY_PIECES = 3
+
+NEGATE_LAG = 1
+TRANSPOSE_LAG = 2
+COMBINE_LAG = 3
+QUANTISE_LAG = 4
+FINISH_LAG = 6
 
 FLOPS = 2 * BATCH * CHANNELS * PIXELS * OUT
 
@@ -47,8 +52,8 @@ def tile_waveletlinearlayer_kernel(tc, x, W_words, W_scales, b, out):
     nc = tc.nc
     with ExitStack() as ctx:
         const = ctx.enter_context(tc.tile_pool(name="const", bufs=1))
-        step1 = ctx.enter_context(tc.tile_pool(name="step1", bufs=4))
-        packed = ctx.enter_context(tc.tile_pool(name="packed", bufs=6))
+        step1 = ctx.enter_context(tc.tile_pool(name="step1", bufs=5))
+        packed = ctx.enter_context(tc.tile_pool(name="packed", bufs=8))
         results = ctx.enter_context(tc.tile_pool(name="results", bufs=2))
         banks = ctx.enter_context(tc.psum_pool(name="banks", bufs=6))
         sums = ctx.enter_context(tc.psum_pool(name="sums", bufs=2))
@@ -85,39 +90,45 @@ def tile_waveletlinearlayer_kernel(tc, x, W_words, W_scales, b, out):
         for piece in range(EARLY_PIECES, STAGES // SIGNS):
             load_pixels(piece)
 
+        def adds_on_vector(stage):
+            return stage % VECTOR_EVERY == VECTOR_EVERY - 1
 
-        def pair_columns(stage, image_row, target):
+        def pair_columns(stage, image_row):
             piece, sign = divmod(stage, SIGNS)
             pairs = pixel_tiles[piece][:].rearrange(
                 "n (i r c t e) -> n r e i c t", i=PASS_ROWS, r=2, c=WORDS_PER_ROW, t=PACK, e=2
             )
+            paired = step1.tile([P, PACK, P], F32, name="paired_%d" % image_row)
             nc.vector.tensor_tensor(
-                out=target[:].rearrange("n t (i c) -> n i c t", c=WORDS_PER_ROW),
+                out=paired[:].rearrange("n t (i c) -> n i c t", c=WORDS_PER_ROW),
                 in0=pairs[:, image_row, 0],
                 in1=pairs[:, image_row, 1],
                 op=(ADD if sign == 0 else SUBTRACT),
             )
+            return paired
 
-        def transpose_and_add(first, second, grouped_slot):
+        def negate(odd):
+            minus_odd = step1.tile([P, PACK, P], F32)
+            nc.scalar.activation(out=minus_odd[:], in_=odd[:], func=COPY, scale=-1.0)
+            return minus_odd
+
+        def transpose_planes(addends):
             bank = banks.tile([P, PACK, P], F32)
             for t in range(PACK):
-                nc.tensor.matmul(
-                    out=bank[:, t, :], lhsT=first[:, t, :], rhs=identity[:],
-                    is_transpose=True, start=True, stop=False,
-                )
-                nc.tensor.matmul(
-                    out=bank[:, t, :], lhsT=second[:, t, :], rhs=identity[:],
-                    is_transpose=True, start=False, stop=True,
-                )
-            nc.scalar.activation(out=grouped_slot, in_=bank[:].rearrange("p t n -> p n t"), func=COPY, scale=0.5)
+                for position, addend in enumerate(addends):
+                    nc.tensor.matmul(
+                        out=bank[:, t, :], lhsT=addend[:, t, :], rhs=identity[:], is_transpose=True,
+                        start=(position == 0), stop=(position == len(addends) - 1),
+                    )
+            return bank
 
-        grouped_tiles = {}
-        sum_tiles = {}
+        def by_word(bank):
+            return bank[:].rearrange("p t n -> p n t")
 
-        code_tiles = {}
+        def halve_out_of_psum(bank, target):
+            nc.scalar.activation(out=target, in_=by_word(bank), func=COPY, scale=0.5)
 
-        def quantise(stage):
-            grouped = grouped_tiles.pop(stage)
+        def quantise(grouped):
             t_codes = packed.tile([P, STAGE_PASSES, P], U32, align_bytes=64)
             t_scales = packed.tile([P, STAGE_PASSES, P], U8, align_bytes=64)
             nc.vector.quantize_mx(
@@ -125,13 +136,14 @@ def tile_waveletlinearlayer_kernel(tc, x, W_words, W_scales, b, out):
                 scales=t_scales[:].rearrange("p s n -> p (s n)"),
                 in_=grouped[:].rearrange("p s n t -> p (s n t)"),
             )
-            code_tiles[stage] = (t_codes, t_scales)
+            return t_codes, t_scales
 
-        def multiply(stage):
+        sum_tiles = {}
+
+        def multiply(stage, t_codes, t_scales):
             row_tile, tile_stage = divmod(stage, TILE_STAGES)
             channel, rest = divmod(tile_stage, BAND_PASSES * SIGNS)
             half, sign = divmod(rest, SIGNS)
-            t_codes, t_scales = code_tiles.pop(stage)
             if tile_stage == 0:
                 sum_tiles[row_tile] = sums.tile([P, OUT], F32, name="batch_sum")
             for difference in range(STAGE_PASSES):
@@ -152,29 +164,60 @@ def tile_waveletlinearlayer_kernel(tc, x, W_words, W_scales, b, out):
             nc.vector.tensor_tensor(out=result[:], in0=sum_tiles[row_tile][:], in1=bias[:], op=ADD)
             nc.sync.dma_start(out=out[row_tile * P : (row_tile + 1) * P, :], in_=result[:])
 
+        evens, odds, minus_odds = {}, {}, {}
+        even_banks, halved_odds = {}, {}
+        grouped_tiles, code_tiles = {}, {}
         waiting = []
-        for step in range(STAGES + FINISH_LAG):
-            if step < STAGES:
-                even = step1.tile([P, PACK, P], F32)
-                odd = step1.tile([P, PACK, P], F32)
-                minus_odd = step1.tile([P, PACK, P], F32)
-                pair_columns(step, 0, even)
-            finished = step - FINISH_LAG
-            if finished >= 0 and (finished + 1) % TILE_STAGES == 0:
-                finish(finished // TILE_STAGES)
-            if step < STAGES:
-                pair_columns(step, 1, odd)
-                nc.scalar.activation(out=minus_odd[:], in_=odd[:], func=COPY, scale=-1.0)
-            quantised = step - QUANTISE_LAG
-            if 0 <= quantised < STAGES:
-                quantise(quantised)
-                waiting.append(quantised)
-                if len(waiting) == RUN_STAGES or step >= STAGES:
-                    for stage in waiting:
-                        multiply(stage)
-                    waiting = []
-            if step < STAGES:
+
+        for turn in range(STAGES + FINISH_LAG + 1):
+            stage = turn - QUANTISE_LAG
+            if 0 <= stage < STAGES:
+                code_tiles[stage] = quantise(grouped_tiles[stage])
+                waiting.append(stage)
+            if turn >= STAGES + TRANSPOSE_LAG:
+                run = len(waiting)
+            elif len(waiting) > RUN_STAGES:
+                run = RUN_STAGES
+            else:
+                run = 0
+            for ready in waiting[:run]:
+                multiply(ready, code_tiles[ready][0], code_tiles[ready][1])
+            waiting = waiting[run:]
+
+            stage = turn - COMBINE_LAG
+            if 0 <= stage < STAGES and adds_on_vector(stage):
+                for difference in range(STAGE_PASSES):
+                    nc.vector.scalar_tensor_tensor(
+                        out=grouped_tiles[stage][:, difference],
+                        in0=by_word(even_banks[stage]),
+                        scalar=0.5,
+                        in1=halved_odds[stage][:],
+                        op0=MULT,
+                        op1=(SUBTRACT if difference else ADD),
+                    )
+
+            stage = turn - FINISH_LAG
+            if stage >= 0 and (stage + 1) % TILE_STAGES == 0:
+                finish(stage // TILE_STAGES)
+
+            stage = turn
+            if stage < STAGES:
+                evens[stage] = pair_columns(stage, 0)
+                odds[stage] = pair_columns(stage, 1)
+
+            stage = turn - NEGATE_LAG
+            if 0 <= stage < STAGES and not adds_on_vector(stage):
+                minus_odds[stage] = negate(odds[stage])
+
+            stage = turn - TRANSPOSE_LAG
+            if 0 <= stage < STAGES:
                 grouped = packed.tile([P, STAGE_PASSES, P, PACK], BF16, align_bytes=64)
-                grouped_tiles[step] = grouped
-                transpose_and_add(even, odd, grouped[:, 0])
-                transpose_and_add(even, minus_odd, grouped[:, 1])
+                grouped_tiles[stage] = grouped
+                if adds_on_vector(stage):
+                    halved_odd = step1.tile([P, P, PACK], F32)
+                    halve_out_of_psum(transpose_planes([odds[stage]]), halved_odd[:])
+                    halved_odds[stage] = halved_odd
+                    even_banks[stage] = transpose_planes([evens[stage]])
+                else:
+                    halve_out_of_psum(transpose_planes([evens[stage], odds[stage]]), grouped[:, 0])
+                    halve_out_of_psum(transpose_planes([evens[stage], minus_odds[stage]]), grouped[:, 1])

@@ -35,8 +35,9 @@ SIGNS = 2
 TILE_STAGES = CHANNELS * BAND_PASSES * SIGNS
 STAGES = ROW_TILES * TILE_STAGES
 STAGE_PASSES = 2
-VECTOR_EVERY = 3
+VECTOR_EVERY = 8
 RUN_STAGES = 4
+KEEP_ALIVE_EVERY = 20
 EARLY_PIECES = 3
 
 NEGATE_LAG = 1
@@ -56,7 +57,8 @@ def tile_waveletlinearlayer_kernel(tc, x, W_words, W_scales, b, out):
         packed = ctx.enter_context(tc.tile_pool(name="packed", bufs=8))
         results = ctx.enter_context(tc.tile_pool(name="results", bufs=2))
         banks = ctx.enter_context(tc.psum_pool(name="banks", bufs=6))
-        sums = ctx.enter_context(tc.psum_pool(name="sums", bufs=2))
+        sums = ctx.enter_context(tc.psum_pool(name="sums", bufs=1))
+        spare = ctx.enter_context(tc.psum_pool(name="spare", bufs=1))
         ctx.enter_context(tc.manual_schedule())
 
         identity = const.tile([P, P], F32)
@@ -112,6 +114,14 @@ def tile_waveletlinearlayer_kernel(tc, x, W_words, W_scales, b, out):
             nc.scalar.activation(out=minus_odd[:], in_=odd[:], func=COPY, scale=-1.0)
             return minus_odd
 
+        unread = spare.tile([P, P], F32)
+        transposes_issued = [0]
+
+        def keep_clock_up():
+            transposes_issued[0] += 1
+            if transposes_issued[0] % KEEP_ALIVE_EVERY == 0:
+                nc.tensor.matmul(out=unread[:], lhsT=identity[:], rhs=identity[:], start=True, stop=True)
+
         def transpose_planes(addends):
             bank = banks.tile([P, PACK, P], F32)
             for t in range(PACK):
@@ -120,6 +130,7 @@ def tile_waveletlinearlayer_kernel(tc, x, W_words, W_scales, b, out):
                         out=bank[:, t, :], lhsT=addend[:, t, :], rhs=identity[:], is_transpose=True,
                         start=(position == 0), stop=(position == len(addends) - 1),
                     )
+                    keep_clock_up()
             return bank
 
         def by_word(bank):

@@ -12,7 +12,6 @@ FP8X4 = mybir.dt.float8_e4m3fn_x4
 FP4X4 = mybir.dt.float4_e2m1fn_x4
 ADD = mybir.AluOpType.add
 SUBTRACT = mybir.AluOpType.subtract
-MULT = mybir.AluOpType.mult
 COPY = mybir.ActivationFunctionType.Copy
 
 P = 128
@@ -30,19 +29,19 @@ PASS_ROWS = HALF_SIDE // BAND_PASSES
 PASS_PIXELS = PIXELS // BAND_PASSES
 ROW_TILES = BATCH // P
 WORDS_PER_ROW = HALF_SIDE // PACK
+EVEN, ODD = 0, 1
 
 SIGNS = 2
 TILE_STAGES = CHANNELS * BAND_PASSES * SIGNS
 STAGES = ROW_TILES * TILE_STAGES
 STAGE_PASSES = 2
-VECTOR_EVERY = 8
 RUN_STAGES = 4
-KEEP_ALIVE_EVERY = 20
+VECTOR_NEGATES_EVERY = 8
+KEEP_ALIVE_EVERY = 21
 EARLY_PIECES = 3
 
 NEGATE_LAG = 1
 TRANSPOSE_LAG = 2
-COMBINE_LAG = 3
 QUANTISE_LAG = 4
 FINISH_LAG = 6
 
@@ -92,26 +91,26 @@ def tile_waveletlinearlayer_kernel(tc, x, W_words, W_scales, b, out):
         for piece in range(EARLY_PIECES, STAGES // SIGNS):
             load_pixels(piece)
 
-        def adds_on_vector(stage):
-            return stage % VECTOR_EVERY == VECTOR_EVERY - 1
-
-        def pair_columns(stage, image_row):
+        def pair_columns(stage):
             piece, sign = divmod(stage, SIGNS)
-            pairs = pixel_tiles[piece][:].rearrange(
-                "n (i r c t e) -> n r e i c t", i=PASS_ROWS, r=2, c=WORDS_PER_ROW, t=PACK, e=2
+            pixels = pixel_tiles[piece][:].rearrange(
+                "n (i r c t e) -> n e r i c t", i=PASS_ROWS, r=2, c=WORDS_PER_ROW, t=PACK, e=2
             )
-            paired = step1.tile([P, PACK, P], F32, name="paired_%d" % image_row)
+            paired = step1.tile([P, 2, PACK, P], F32)
             nc.vector.tensor_tensor(
-                out=paired[:].rearrange("n t (i c) -> n i c t", c=WORDS_PER_ROW),
-                in0=pairs[:, image_row, 0],
-                in1=pairs[:, image_row, 1],
+                out=paired[:].rearrange("n r t (i c) -> n r i c t", c=WORDS_PER_ROW),
+                in0=pixels[:, 0],
+                in1=pixels[:, 1],
                 op=(ADD if sign == 0 else SUBTRACT),
             )
             return paired
 
-        def negate(odd):
+        def negate(stage, odd):
             minus_odd = step1.tile([P, PACK, P], F32)
-            nc.scalar.activation(out=minus_odd[:], in_=odd[:], func=COPY, scale=-1.0)
+            if stage % VECTOR_NEGATES_EVERY == VECTOR_NEGATES_EVERY - 1:
+                nc.vector.tensor_scalar_mul(out=minus_odd[:], in0=odd, scalar1=-1.0)
+            else:
+                nc.scalar.activation(out=minus_odd[:], in_=odd, func=COPY, scale=-1.0)
             return minus_odd
 
         unread = spare.tile([P, P], F32)
@@ -122,22 +121,16 @@ def tile_waveletlinearlayer_kernel(tc, x, W_words, W_scales, b, out):
             if transposes_issued[0] % KEEP_ALIVE_EVERY == 0:
                 nc.tensor.matmul(out=unread[:], lhsT=identity[:], rhs=identity[:], start=True, stop=True)
 
-        def transpose_planes(addends):
+        def transpose_and_add(first, second, target):
             bank = banks.tile([P, PACK, P], F32)
             for t in range(PACK):
-                for position, addend in enumerate(addends):
+                for addend in (first, second):
                     nc.tensor.matmul(
                         out=bank[:, t, :], lhsT=addend[:, t, :], rhs=identity[:], is_transpose=True,
-                        start=(position == 0), stop=(position == len(addends) - 1),
+                        start=(addend is first), stop=(addend is second),
                     )
                     keep_clock_up()
-            return bank
-
-        def by_word(bank):
-            return bank[:].rearrange("p t n -> p n t")
-
-        def halve_out_of_psum(bank, target):
-            nc.scalar.activation(out=target, in_=by_word(bank), func=COPY, scale=0.5)
+            nc.scalar.activation(out=target, in_=bank[:].rearrange("p t n -> p n t"), func=COPY, scale=0.5)
 
         def quantise(grouped):
             t_codes = packed.tile([P, STAGE_PASSES, P], U32, align_bytes=64)
@@ -175,9 +168,7 @@ def tile_waveletlinearlayer_kernel(tc, x, W_words, W_scales, b, out):
             nc.vector.tensor_tensor(out=result[:], in0=sum_tiles[row_tile][:], in1=bias[:], op=ADD)
             nc.sync.dma_start(out=out[row_tile * P : (row_tile + 1) * P, :], in_=result[:])
 
-        evens, odds, minus_odds = {}, {}, {}
-        even_banks, halved_odds = {}, {}
-        grouped_tiles, code_tiles = {}, {}
+        paired_tiles, minus_odds, grouped_tiles, code_tiles = {}, {}, {}, {}
         waiting = []
 
         for turn in range(STAGES + FINISH_LAG + 1):
@@ -195,40 +186,22 @@ def tile_waveletlinearlayer_kernel(tc, x, W_words, W_scales, b, out):
                 multiply(ready, code_tiles[ready][0], code_tiles[ready][1])
             waiting = waiting[run:]
 
-            stage = turn - COMBINE_LAG
-            if 0 <= stage < STAGES and adds_on_vector(stage):
-                for difference in range(STAGE_PASSES):
-                    nc.vector.scalar_tensor_tensor(
-                        out=grouped_tiles[stage][:, difference],
-                        in0=by_word(even_banks[stage]),
-                        scalar=0.5,
-                        in1=halved_odds[stage][:],
-                        op0=MULT,
-                        op1=(SUBTRACT if difference else ADD),
-                    )
-
             stage = turn - FINISH_LAG
             if stage >= 0 and (stage + 1) % TILE_STAGES == 0:
                 finish(stage // TILE_STAGES)
 
             stage = turn
             if stage < STAGES:
-                evens[stage] = pair_columns(stage, 0)
-                odds[stage] = pair_columns(stage, 1)
+                paired_tiles[stage] = pair_columns(stage)
 
             stage = turn - NEGATE_LAG
-            if 0 <= stage < STAGES and not adds_on_vector(stage):
-                minus_odds[stage] = negate(odds[stage])
+            if 0 <= stage < STAGES:
+                minus_odds[stage] = negate(stage, paired_tiles[stage][:, ODD])
 
             stage = turn - TRANSPOSE_LAG
             if 0 <= stage < STAGES:
+                even, odd = paired_tiles[stage][:, EVEN], paired_tiles[stage][:, ODD]
                 grouped = packed.tile([P, STAGE_PASSES, P, PACK], BF16, align_bytes=64)
                 grouped_tiles[stage] = grouped
-                if adds_on_vector(stage):
-                    halved_odd = step1.tile([P, P, PACK], F32)
-                    halve_out_of_psum(transpose_planes([odds[stage]]), halved_odd[:])
-                    halved_odds[stage] = halved_odd
-                    even_banks[stage] = transpose_planes([evens[stage]])
-                else:
-                    halve_out_of_psum(transpose_planes([evens[stage], odds[stage]]), grouped[:, 0])
-                    halve_out_of_psum(transpose_planes([evens[stage], minus_odds[stage]]), grouped[:, 1])
+                transpose_and_add(even, odd, grouped[:, 0])
+                transpose_and_add(even, minus_odds[stage][:], grouped[:, 1])

@@ -37,7 +37,7 @@ STAGES = ROW_TILES * TILE_STAGES
 STAGE_PASSES = 2
 RUN_STAGES = 4
 VECTOR_NEGATES_EVERY = 8
-KEEP_ALIVE_EVERY = 21
+KEEP_ALIVE_EVERY = 32
 EARLY_PIECES = 3
 
 NEGATE_LAG = 1

@@ -36,8 +36,7 @@ TILE_STAGES = CHANNELS * BAND_PASSES * SIGNS
 STAGES = ROW_TILES * TILE_STAGES
 STAGE_PASSES = 2
 RUN_STAGES = 4
-VECTOR_NEGATES_EVERY = 8
-KEEP_ALIVE_EVERY = 32
+KEEP_ALIVE_EVERY = 21
 EARLY_PIECES = 3
 
 NEGATE_LAG = 1
@@ -105,12 +104,9 @@ def tile_waveletlinearlayer_kernel(tc, x, W_words, W_scales, b, out):
             )
             return paired
 
-        def negate(stage, odd):
+        def negate(odd):
             minus_odd = step1.tile([P, PACK, P], F32)
-            if stage % VECTOR_NEGATES_EVERY == VECTOR_NEGATES_EVERY - 1:
-                nc.vector.tensor_scalar_mul(out=minus_odd[:], in0=odd, scalar1=-1.0)
-            else:
-                nc.scalar.activation(out=minus_odd[:], in_=odd, func=COPY, scale=-1.0)
+            nc.scalar.activation(out=minus_odd[:], in_=odd, func=COPY, scale=-1.0)
             return minus_odd
 
         unread = spare.tile([P, P], F32)
@@ -196,7 +192,7 @@ def tile_waveletlinearlayer_kernel(tc, x, W_words, W_scales, b, out):
 
             stage = turn - NEGATE_LAG
             if 0 <= stage < STAGES:
-                minus_odds[stage] = negate(stage, paired_tiles[stage][:, ODD])
+                minus_odds[stage] = negate(paired_tiles[stage][:, ODD])
 
             stage = turn - TRANSPOSE_LAG
             if 0 <= stage < STAGES:

@@ -37,7 +37,7 @@ STAGES = ROW_TILES * TILE_STAGES
 STAGE_PASSES = 2
 RUN_STAGES = 4
 KEEP_ALIVE_EVERY = 21
-EARLY_PIECES = 3
+EARLY_PIECES = 5
 
 NEGATE_LAG = 1
 TRANSPOSE_LAG = 2
@@ -86,9 +86,9 @@ def tile_waveletlinearlayer_kernel(tc, x, W_words, W_scales, b, out):
                 in_=W_scales[:, 4 * quadrant : 4 * quadrant + 4, :].bitcast(I32).rearrange("g r w -> r g w"),
             )
         nc.sync.dma_start(out=w_codes[:].bitcast(I32), in_=W_words.bitcast(I32).rearrange("g p w -> p g w"))
-        nc.sync.dma_start(out=bias[:], in_=b.partition_broadcast(P))
         for piece in range(EARLY_PIECES, STAGES // SIGNS):
             load_pixels(piece)
+        nc.sync.dma_start(out=bias[:], in_=b.partition_broadcast(P))
 
         def pair_columns(stage):
             piece, sign = divmod(stage, SIGNS)

@@ -35,9 +35,10 @@ SIGNS = 2
 TILE_STAGES = CHANNELS * BAND_PASSES * SIGNS
 STAGES = ROW_TILES * TILE_STAGES
 STAGE_PASSES = 2
-RUN_STAGES = 4
+RUN_STAGES = 8
 KEEP_ALIVE_EVERY = 21
 EARLY_PIECES = 5
+HEAD_CHUNKS = 4
 
 NEGATE_LAG = 1
 TRANSPOSE_LAG = 2
@@ -52,7 +53,7 @@ def tile_waveletlinearlayer_kernel(tc, x, W_words, W_scales, b, out):
     with ExitStack() as ctx:
         const = ctx.enter_context(tc.tile_pool(name="const", bufs=1))
         step1 = ctx.enter_context(tc.tile_pool(name="step1", bufs=5))
-        packed = ctx.enter_context(tc.tile_pool(name="packed", bufs=8))
+        packed = ctx.enter_context(tc.tile_pool(name="packed", bufs=14))
         results = ctx.enter_context(tc.tile_pool(name="results", bufs=2))
         banks = ctx.enter_context(tc.psum_pool(name="banks", bufs=6))
         sums = ctx.enter_context(tc.psum_pool(name="sums", bufs=1))
@@ -66,12 +67,14 @@ def tile_waveletlinearlayer_kernel(tc, x, W_words, W_scales, b, out):
 
         def load_pixels(piece):
             row_tile, columns = divmod(piece, CHANNELS * BAND_PASSES)
-            pixels = const.tile([P, PASS_PIXELS], BF16, name="pixels_%d" % piece)
-            nc.sync.dma_start(
-                out=pixels[:],
-                in_=x[row_tile * P : (row_tile + 1) * P, columns * PASS_PIXELS : (columns + 1) * PASS_PIXELS],
-            )
-            pixel_tiles[piece] = pixels
+            chunks = HEAD_CHUNKS if piece == 0 else 1
+            width = PASS_PIXELS // chunks
+            pixel_tiles[piece] = []
+            for chunk in range(chunks):
+                pixels = const.tile([P, width], BF16, name="pixels_%d_%d" % (piece, chunk))
+                first = columns * PASS_PIXELS + chunk * width
+                nc.sync.dma_start(out=pixels[:], in_=x[row_tile * P : (row_tile + 1) * P, first : first + width])
+                pixel_tiles[piece].append(pixels)
 
         w_scales = const.tile([P, PASSES, OUT], U8, align_bytes=64)
         nc.vector.memset(w_scales[:].bitcast(I32), 0)
@@ -92,16 +95,19 @@ def tile_waveletlinearlayer_kernel(tc, x, W_words, W_scales, b, out):
 
         def pair_columns(stage):
             piece, sign = divmod(stage, SIGNS)
-            pixels = pixel_tiles[piece][:].rearrange(
-                "n (i r c t e) -> n e r i c t", i=PASS_ROWS, r=2, c=WORDS_PER_ROW, t=PACK, e=2
-            )
             paired = step1.tile([P, 2, PACK, P], F32)
-            nc.vector.tensor_tensor(
-                out=paired[:].rearrange("n r t (i c) -> n r i c t", c=WORDS_PER_ROW),
-                in0=pixels[:, 0],
-                in1=pixels[:, 1],
-                op=(ADD if sign == 0 else SUBTRACT),
-            )
+            planes = paired[:].rearrange("n r t (i c) -> n r i c t", c=WORDS_PER_ROW)
+            rows = PASS_ROWS // len(pixel_tiles[piece])
+            for chunk, chunk_tile in enumerate(pixel_tiles[piece]):
+                pixels = chunk_tile[:].rearrange(
+                    "n (i r c t e) -> n e r i c t", i=rows, r=2, c=WORDS_PER_ROW, t=PACK, e=2
+                )
+                nc.vector.tensor_tensor(
+                    out=planes[:, :, chunk * rows : (chunk + 1) * rows],
+                    in0=pixels[:, 0],
+                    in1=pixels[:, 1],
+                    op=(ADD if sign == 0 else SUBTRACT),
+                )
             return paired
 
         def negate(odd):

@@ -36,7 +36,7 @@ TILE_STAGES = CHANNELS * BAND_PASSES * SIGNS
 STAGES = ROW_TILES * TILE_STAGES
 STAGE_PASSES = 2
 RUN_STAGES = 8
-KEEP_ALIVE_EVERY = 21
+MATMUL_STAGES_OF = 4
 EARLY_PIECES = 5
 HEAD_CHUNKS = 4
 
@@ -57,7 +57,6 @@ def tile_waveletlinearlayer_kernel(tc, x, W_words, W_scales, b, out):
         results = ctx.enter_context(tc.tile_pool(name="results", bufs=2))
         banks = ctx.enter_context(tc.psum_pool(name="banks", bufs=6))
         sums = ctx.enter_context(tc.psum_pool(name="sums", bufs=1))
-        spare = ctx.enter_context(tc.psum_pool(name="spare", bufs=1))
         ctx.enter_context(tc.manual_schedule())
 
         identity = const.tile([P, P], F32)
@@ -78,6 +77,8 @@ def tile_waveletlinearlayer_kernel(tc, x, W_words, W_scales, b, out):
 
         w_scales = const.tile([P, PASSES, OUT], U8, align_bytes=64)
         nc.vector.memset(w_scales[:].bitcast(I32), 0)
+        minus_identity = const.tile([P, P], F32)
+        nc.vector.tensor_scalar_mul(out=minus_identity[:], in0=identity[:], scalar1=-1.0)
         w_codes = const.tile([P, PASSES, 2 * OUT], U8, align_bytes=64)
         bias = const.tile([P, OUT], BF16)
 
@@ -110,28 +111,30 @@ def tile_waveletlinearlayer_kernel(tc, x, W_words, W_scales, b, out):
                 )
             return paired
 
-        def negate(odd):
+        def negated_planes(stage):
+            return PACK if stage % MATMUL_STAGES_OF == MATMUL_STAGES_OF - 1 else PACK - 1
+
+        def negate(stage, odd):
             minus_odd = step1.tile([P, PACK, P], F32)
-            nc.scalar.activation(out=minus_odd[:], in_=odd, func=COPY, scale=-1.0)
+            planes = negated_planes(stage)
+            nc.scalar.activation(out=minus_odd[:, :planes], in_=odd[:, :planes], func=COPY, scale=-1.0)
             return minus_odd
 
-        unread = spare.tile([P, P], F32)
-        transposes_issued = [0]
-
-        def keep_clock_up():
-            transposes_issued[0] += 1
-            if transposes_issued[0] % KEEP_ALIVE_EVERY == 0:
-                nc.tensor.matmul(out=unread[:], lhsT=identity[:], rhs=identity[:], start=True, stop=True)
-
-        def transpose_and_add(first, second, target):
+        def transpose_and_add(first, second, target, subtracted=None, transposed_planes=PACK):
             bank = banks.tile([P, PACK, P], F32)
             for t in range(PACK):
-                for addend in (first, second):
+                nc.tensor.matmul(
+                    out=bank[:, t, :], lhsT=first[:, t, :], rhs=identity[:], is_transpose=True, start=True, stop=False
+                )
+                if t < transposed_planes:
                     nc.tensor.matmul(
-                        out=bank[:, t, :], lhsT=addend[:, t, :], rhs=identity[:], is_transpose=True,
-                        start=(addend is first), stop=(addend is second),
+                        out=bank[:, t, :], lhsT=second[:, t, :], rhs=identity[:], is_transpose=True,
+                        start=False, stop=True,
                     )
-                    keep_clock_up()
+                else:
+                    nc.tensor.matmul(
+                        out=bank[:, t, :], lhsT=subtracted[:, t, :], rhs=minus_identity[:], start=False, stop=True
+                    )
             nc.scalar.activation(out=target, in_=bank[:].rearrange("p t n -> p n t"), func=COPY, scale=0.5)
 
         def quantise(grouped):
@@ -198,7 +201,7 @@ def tile_waveletlinearlayer_kernel(tc, x, W_words, W_scales, b, out):
 
             stage = turn - NEGATE_LAG
             if 0 <= stage < STAGES:
-                minus_odds[stage] = negate(paired_tiles[stage][:, ODD])
+                minus_odds[stage] = negate(stage, paired_tiles[stage][:, ODD])
 
             stage = turn - TRANSPOSE_LAG
             if 0 <= stage < STAGES:
@@ -206,4 +209,6 @@ def tile_waveletlinearlayer_kernel(tc, x, W_words, W_scales, b, out):
                 grouped = packed.tile([P, STAGE_PASSES, P, PACK], BF16, align_bytes=64)
                 grouped_tiles[stage] = grouped
                 transpose_and_add(even, odd, grouped[:, 0])
-                transpose_and_add(even, minus_odds[stage][:], grouped[:, 1])
+                transpose_and_add(
+                    even, minus_odds[stage][:], grouped[:, 1], subtracted=odd, transposed_planes=negated_planes(stage)
+                )

from contextlib import ExitStack

import concourse.mybir as mybir
from concourse.masks import make_identity

F32 = mybir.dt.float32
BF16 = mybir.dt.bfloat16
I32 = mybir.dt.int32
U32 = mybir.dt.uint32
U8 = mybir.dt.uint8
FP8X4 = mybir.dt.float8_e4m3fn_x4
FP4X4 = mybir.dt.float4_e2m1fn_x4
ADD = mybir.AluOpType.add
SUBTRACT = mybir.AluOpType.subtract
COPY = mybir.ActivationFunctionType.Copy

P = 128
PACK = 4
K_PASS = P * PACK

BATCH, CHANNELS, SIDE, OUT = 256, 4, 64, 128
HALF_SIDE = SIDE // 2
PIXELS = SIDE * SIDE
BAND = HALF_SIDE * HALF_SIDE
SUBBANDS = 4
PASSES = CHANNELS * SUBBANDS * BAND // K_PASS
BAND_PASSES = BAND // K_PASS
PASS_ROWS = HALF_SIDE // BAND_PASSES
PASS_PIXELS = PIXELS // BAND_PASSES
ROW_TILES = BATCH // P
WORDS_PER_ROW = HALF_SIDE // PACK
EVEN, ODD = 0, 1

SIGNS = 2
TILE_STAGES = CHANNELS * BAND_PASSES * SIGNS
STAGES = ROW_TILES * TILE_STAGES
STAGE_PASSES = 2
RUN_STAGES = 8
MATMUL_STAGES_OF = 4
EARLY_PIECES = 5
HEAD_CHUNKS = 4

NEGATE_LAG = 1
TRANSPOSE_LAG = 2
QUANTISE_LAG = 4
FINISH_LAG = 6

FLOPS = 2 * BATCH * CHANNELS * PIXELS * OUT


def tile_waveletlinearlayer_kernel(tc, x, W_words, W_scales, b, out):
    nc = tc.nc
    with ExitStack() as ctx:
        const = ctx.enter_context(tc.tile_pool(name="const", bufs=1))
        step1 = ctx.enter_context(tc.tile_pool(name="step1", bufs=5))
        packed = ctx.enter_context(tc.tile_pool(name="packed", bufs=14))
        results = ctx.enter_context(tc.tile_pool(name="results", bufs=2))
        banks = ctx.enter_context(tc.psum_pool(name="banks", bufs=6))
        sums = ctx.enter_context(tc.psum_pool(name="sums", bufs=1))
        ctx.enter_context(tc.manual_schedule())

        identity = const.tile([P, P], F32)
        make_identity(nc, identity[:])

        pixel_tiles = {}

        def load_pixels(piece):
            row_tile, columns = divmod(piece, CHANNELS * BAND_PASSES)
            chunks = HEAD_CHUNKS if piece == 0 else 1
            width = PASS_PIXELS // chunks
            pixel_tiles[piece] = []
            for chunk in range(chunks):
                pixels = const.tile([P, width], BF16, name="pixels_%d_%d" % (piece, chunk))
                first = columns * PASS_PIXELS + chunk * width
                nc.sync.dma_start(out=pixels[:], in_=x[row_tile * P : (row_tile + 1) * P, first : first + width])
                pixel_tiles[piece].append(pixels)

        w_scales = const.tile([P, PASSES, OUT], U8, align_bytes=64)
        nc.vector.memset(w_scales[:].bitcast(I32), 0)
        minus_identity = const.tile([P, P], F32)
        nc.vector.tensor_scalar_mul(out=minus_identity[:], in0=identity[:], scalar1=-1.0)
        w_codes = const.tile([P, PASSES, 2 * OUT], U8, align_bytes=64)
        bias = const.tile([P, OUT], BF16)

        for piece in range(EARLY_PIECES):
            load_pixels(piece)
        for quadrant in range(4):
            nc.sync.dma_start(
                out=w_scales[32 * quadrant : 32 * quadrant + 4].bitcast(I32),
                in_=W_scales[:, 4 * quadrant : 4 * quadrant + 4, :].bitcast(I32).rearrange("g r w -> r g w"),
            )
        nc.sync.dma_start(out=w_codes[:].bitcast(I32), in_=W_words.bitcast(I32).rearrange("g p w -> p g w"))
        for piece in range(EARLY_PIECES, STAGES // SIGNS):
            load_pixels(piece)
        nc.sync.dma_start(out=bias[:], in_=b.partition_broadcast(P))

        def pair_columns(stage):
            piece, sign = divmod(stage, SIGNS)
            paired = step1.tile([P, 2, PACK, P], F32)
            planes = paired[:].rearrange("n r t (i c) -> n r i c t", c=WORDS_PER_ROW)
            rows = PASS_ROWS // len(pixel_tiles[piece])
            for chunk, chunk_tile in enumerate(pixel_tiles[piece]):
                pixels = chunk_tile[:].rearrange(
                    "n (i r c t e) -> n e r i c t", i=rows, r=2, c=WORDS_PER_ROW, t=PACK, e=2
                )
                nc.vector.tensor_tensor(
                    out=planes[:, :, chunk * rows : (chunk + 1) * rows],
                    in0=pixels[:, 0],
                    in1=pixels[:, 1],
                    op=(ADD if sign == 0 else SUBTRACT),
                )
            return paired

        def negated_planes(stage):
            return PACK if stage % MATMUL_STAGES_OF == MATMUL_STAGES_OF - 1 else PACK - 1

        def negate(stage, odd):
            minus_odd = step1.tile([P, PACK, P], F32)
            planes = negated_planes(stage)
            nc.scalar.activation(out=minus_odd[:, :planes], in_=odd[:, :planes], func=COPY, scale=-1.0)
            return minus_odd

        def transpose_and_add(first, second, target, subtracted=None, transposed_planes=PACK):
            bank = banks.tile([P, PACK, P], F32)
            for t in range(PACK):
                nc.tensor.matmul(
                    out=bank[:, t, :], lhsT=first[:, t, :], rhs=identity[:], is_transpose=True, start=True, stop=False
                )
                if t < transposed_planes:
                    nc.tensor.matmul(
                        out=bank[:, t, :], lhsT=second[:, t, :], rhs=identity[:], is_transpose=True,
                        start=False, stop=True,
                    )
                else:
                    nc.tensor.matmul(
                        out=bank[:, t, :], lhsT=subtracted[:, t, :], rhs=minus_identity[:], start=False, stop=True
                    )
            nc.scalar.activation(out=target, in_=bank[:].rearrange("p t n -> p n t"), func=COPY, scale=0.5)

        def quantise(grouped):
            t_codes = packed.tile([P, STAGE_PASSES, P], U32, align_bytes=64)
            t_scales = packed.tile([P, STAGE_PASSES, P], U8, align_bytes=64)
            nc.vector.quantize_mx(
                out=t_codes[:].rearrange("p s n -> p (s n)").bitcast(FP8X4),
                scales=t_scales[:].rearrange("p s n -> p (s n)"),
                in_=grouped[:].rearrange("p s n t -> p (s n t)"),
            )
            return t_codes, t_scales

        sum_tiles = {}

        def multiply(stage, t_codes, t_scales):
            row_tile, tile_stage = divmod(stage, TILE_STAGES)
            channel, rest = divmod(tile_stage, BAND_PASSES * SIGNS)
            half, sign = divmod(rest, SIGNS)
            if tile_stage == 0:
                sum_tiles[row_tile] = sums.tile([P, OUT], F32, name="batch_sum")
            for difference in range(STAGE_PASSES):
                subband = 2 * sign + difference
                g = (channel * SUBBANDS + subband) * BAND_PASSES + half
                nc.tensor.matmul_mx(
                    out=sum_tiles[row_tile][:],
                    lhsT=t_codes[:, difference, :].bitcast(FP8X4),
                    lhsT_scale=t_scales[:, difference, :],
                    rhs=w_codes[:, g, :].bitcast(FP4X4),
                    rhs_scale=w_scales[:, g, :],
                    start=(tile_stage == 0 and difference == 0),
                    stop=(tile_stage == TILE_STAGES - 1 and difference == STAGE_PASSES - 1),
                )

        def finish(row_tile):
            result = results.tile([P, OUT], F32)
            nc.vector.tensor_tensor(out=result[:], in0=sum_tiles[row_tile][:], in1=bias[:], op=ADD)
            nc.sync.dma_start(out=out[row_tile * P : (row_tile + 1) * P, :], in_=result[:])

        paired_tiles, minus_odds, grouped_tiles, code_tiles = {}, {}, {}, {}
        waiting = []

        for turn in range(STAGES + FINISH_LAG + 1):
            stage = turn - QUANTISE_LAG
            if 0 <= stage < STAGES:
                code_tiles[stage] = quantise(grouped_tiles[stage])
                waiting.append(stage)
            if turn >= STAGES + TRANSPOSE_LAG:
                run = len(waiting)
            elif len(waiting) > RUN_STAGES:
                run = RUN_STAGES
            else:
                run = 0
            for ready in waiting[:run]:
                multiply(ready, code_tiles[ready][0], code_tiles[ready][1])
            waiting = waiting[run:]

            stage = turn - FINISH_LAG
            if stage >= 0 and (stage + 1) % TILE_STAGES == 0:
                finish(stage // TILE_STAGES)

            stage = turn
            if stage < STAGES:
                paired_tiles[stage] = pair_columns(stage)

            stage = turn - NEGATE_LAG
            if 0 <= stage < STAGES:
                minus_odds[stage] = negate(stage, paired_tiles[stage][:, ODD])

            stage = turn - TRANSPOSE_LAG
            if 0 <= stage < STAGES:
                even, odd = paired_tiles[stage][:, EVEN], paired_tiles[stage][:, ODD]
                grouped = packed.tile([P, STAGE_PASSES, P, PACK], BF16, align_bytes=64)
                grouped_tiles[stage] = grouped
                transpose_and_add(even, odd, grouped[:, 0])
                transpose_and_add(
                    even, minus_odds[stage][:], grouped[:, 1], subtracted=odd, transposed_planes=negated_planes(stage)
                )
